import numpy as np
import ml_dtypes

BF16 = ml_dtypes.bfloat16


def bf(x):
    return np.asarray(x, np.float32).astype(BF16)


def f32(x):
    return np.asarray(x, np.float32)


def f64(x):
    return np.asarray(x).astype(np.float64)


def striped(idx):
    return np.tile(idx.reshape(-1, 16).T, (8, 1))


C, S, N = 1024, 1024, 128
EPS = 1e-5


def setup_inputs():
    x = np.random.standard_normal((C, S)) * np.random.uniform(0.5, 2.0, (C, 1))
    return {"x": f32(x), "lnw": f32(1.0 + 0.1 * np.random.standard_normal((1, N))), "offs": striped(np.random.permutation(S)[:N])}


def reference(x, lnw, offs):
    idx = offs[:16].T.reshape(-1)
    xx = f64(x)
    r = 1.0 / np.sqrt(np.mean(xx ** 2, axis=1, keepdims=True) + EPS)
    return xx[:, idx] * f64(lnw) * r

@@ -1,0 +1,50 @@
+import concourse.mybir as mybir
+
+F32 = mybir.dt.float32
+U16 = mybir.dt.uint16
+ACT = mybir.ActivationFunctionType
+MULT = mybir.AluOpType.mult
+
+P = 128
+TOKENS = 1024
+CHANNELS = 1024
+PICKED = 128
+BLOCKS = TOKENS // P
+EPS = 1e-5
+
+
+def tile_qllamadecoderlayer_kernel(tc, x, lnw, offs, out):
+    nc = tc.nc
+    with (
+        tc.tile_pool(name="held", bufs=1) as held,
+        tc.tile_pool(name="tokens", bufs=BLOCKS) as tokens,
+        tc.tile_pool(name="work", bufs=2) as work,
+        tc.tile_pool(name="stats", bufs=BLOCKS) as stats,
+    ):
+        offsets = held.tile([P, PICKED // 16], U16, name="offsets")
+        nc.sync.dma_start(offsets[:], offs)
+        gain = held.tile([P, PICKED], F32, name="gain")
+        nc.scalar.dma_start(gain[:], lnw.broadcast_to([P, PICKED]))
+        eps = held.tile([P, 1], F32, name="eps")
+        nc.vector.memset(eps[:], EPS)
+
+        blocks = []
+        for b in range(BLOCKS):
+            block = tokens.tile([P, CHANNELS], F32, name="block")
+            nc.sync.dma_start(block[:], x[b * P : (b + 1) * P, :])
+            blocks.append(block)
+
+        for b in range(BLOCKS):
+            block = blocks[b]
+            squares = work.tile([P, CHANNELS], F32, name="squares")
+            mean_sq = stats.tile([P, 1], F32, name="mean_sq")
+            nc.scalar.activation(squares[:], block[:], ACT.Square, scale=1.0 / 32.0, accum_out=mean_sq[:])
+            picked = work.tile([P, PICKED], F32, name="picked")
+            nc.vector.tensor_tensor(picked[:], block[:].indirect(offsets[:]), gain[:], MULT)
+            rms = stats.tile([P, 1], F32, name="rms")
+            nc.scalar.activation(rms[:], mean_sq[:], ACT.Sqrt, bias=eps[:])
+            r = stats.tile([P, 1], F32, name="r")
+            nc.vector.reciprocal(r[:], rms[:])
+            result = work.tile([P, PICKED], F32, name="result")
+            nc.vector.tensor_scalar_mul(result[:], picked[:], r[:])
+            nc.sync.dma_start(out[b * P : (b + 1) * P, :], result[:])

@@ -18,7 +18,8 @@ def tile_qllamadecoderlayer_kernel(tc, x, lnw, offs, out):
     with (
         tc.tile_pool(name="held", bufs=1) as held,
         tc.tile_pool(name="tokens", bufs=BLOCKS) as tokens,
-        tc.tile_pool(name="work", bufs=2) as work,
+        tc.tile_pool(name="scratch", bufs=2) as scratch,
+        tc.tile_pool(name="work", bufs=BLOCKS) as work,
         tc.tile_pool(name="stats", bufs=BLOCKS) as stats,
     ):
         offsets = held.tile([P, PICKED // 16], U16, name="offsets")
@@ -36,7 +37,7 @@ def tile_qllamadecoderlayer_kernel(tc, x, lnw, offs, out):
 
         for b in range(BLOCKS):
             block = blocks[b]
-            squares = work.tile([P, CHANNELS], F32, name="squares")
+            squares = scratch.tile([P, CHANNELS], F32, name="squares")
             mean_sq = stats.tile([P, 1], F32, name="mean_sq")
             nc.scalar.activation(squares[:], block[:], ACT.Square, scale=1.0 / 32.0, accum_out=mean_sq[:])
             picked = work.tile([P, PICKED], F32, name="picked")

@@ -11,6 +11,8 @@ CHANNELS = 1024
 PICKED = 128
 BLOCKS = TOKENS // P
 EPS = 1e-5
+SCALAR_SHARE = 3 * CHANNELS // 4
+VECTOR_SHARE = CHANNELS - SCALAR_SHARE
 
 
 def tile_qllamadecoderlayer_kernel(tc, x, lnw, offs, out):
@@ -26,8 +28,6 @@ def tile_qllamadecoderlayer_kernel(tc, x, lnw, offs, out):
         nc.sync.dma_start(offsets[:], offs)
         gain = held.tile([P, PICKED], F32, name="gain")
         nc.scalar.dma_start(gain[:], lnw.broadcast_to([P, PICKED]))
-        eps = held.tile([P, 1], F32, name="eps")
-        nc.vector.memset(eps[:], EPS)
 
         blocks = []
         for b in range(BLOCKS):
@@ -37,13 +37,23 @@ def tile_qllamadecoderlayer_kernel(tc, x, lnw, offs, out):
 
         for b in range(BLOCKS):
             block = blocks[b]
-            squares = scratch.tile([P, CHANNELS], F32, name="squares")
-            mean_sq = stats.tile([P, 1], F32, name="mean_sq")
-            nc.scalar.activation(squares[:], block[:], ACT.Square, scale=1.0 / 32.0, accum_out=mean_sq[:])
+            squares_s = scratch.tile([P, SCALAR_SHARE], F32, name="squares_s")
+            mean_s = stats.tile([P, 1], F32, name="mean_s")
+            nc.scalar.activation(
+                squares_s[:], block[:, :SCALAR_SHARE], ACT.Square, scale=1.0 / 32.0, accum_out=mean_s[:]
+            )
             picked = work.tile([P, PICKED], F32, name="picked")
             nc.vector.tensor_tensor(picked[:], block[:].indirect(offsets[:]), gain[:], MULT)
+            squares_v = scratch.tile([P, VECTOR_SHARE], F32, name="squares_v")
+            mean_v = stats.tile([P, 1], F32, name="mean_v")
+            nc.vector.scalar_tensor_tensor(
+                squares_v[:], block[:, SCALAR_SHARE:], 1.0 / CHANNELS, block[:, SCALAR_SHARE:], MULT, MULT,
+                accum_out=mean_v[:],
+            )
+            mean_v_eps = stats.tile([P, 1], F32, name="mean_v_eps")
+            nc.vector.tensor_scalar_add(mean_v_eps[:], mean_v[:], EPS)
             rms = stats.tile([P, 1], F32, name="rms")
-            nc.scalar.activation(rms[:], mean_sq[:], ACT.Sqrt, bias=eps[:])
+            nc.scalar.activation(rms[:], mean_s[:], ACT.Sqrt, bias=mean_v_eps[:])
             r = stats.tile([P, 1], F32, name="r")
             nc.vector.reciprocal(r[:], rms[:])
             result = work.tile([P, PICKED], F32, name="result")

@@ -11,7 +11,7 @@ CHANNELS = 1024
 PICKED = 128
 BLOCKS = TOKENS // P
 EPS = 1e-5
-SCALAR_SHARE = 3 * CHANNELS // 4
+SCALAR_SHARE = 5 * CHANNELS // 8
 VECTOR_SHARE = CHANNELS - SCALAR_SHARE
 
 
@@ -37,13 +37,6 @@ def tile_qllamadecoderlayer_kernel(tc, x, lnw, offs, out):
 
         for b in range(BLOCKS):
             block = blocks[b]
-            squares_s = scratch.tile([P, SCALAR_SHARE], F32, name="squares_s")
-            mean_s = stats.tile([P, 1], F32, name="mean_s")
-            nc.scalar.activation(
-                squares_s[:], block[:, :SCALAR_SHARE], ACT.Square, scale=1.0 / 32.0, accum_out=mean_s[:]
-            )
-            picked = work.tile([P, PICKED], F32, name="picked")
-            nc.vector.tensor_tensor(picked[:], block[:].indirect(offsets[:]), gain[:], MULT)
             squares_v = scratch.tile([P, VECTOR_SHARE], F32, name="squares_v")
             mean_v = stats.tile([P, 1], F32, name="mean_v")
             nc.vector.scalar_tensor_tensor(
@@ -52,10 +45,16 @@ def tile_qllamadecoderlayer_kernel(tc, x, lnw, offs, out):
             )
             mean_v_eps = stats.tile([P, 1], F32, name="mean_v_eps")
             nc.vector.tensor_scalar_add(mean_v_eps[:], mean_v[:], EPS)
-            rms = stats.tile([P, 1], F32, name="rms")
-            nc.scalar.activation(rms[:], mean_s[:], ACT.Sqrt, bias=mean_v_eps[:])
+            picked = work.tile([P, PICKED], F32, name="picked")
+            nc.vector.tensor_tensor(picked[:], block[:].indirect(offsets[:]), gain[:], MULT)
+
+            squares_s = scratch.tile([P, SCALAR_SHARE], F32, name="squares_s")
+            mean_s = stats.tile([P, 1], F32, name="mean_s")
+            nc.scalar.activation(
+                squares_s[:], block[:, :SCALAR_SHARE], ACT.Square, scale=1.0 / 32.0, accum_out=mean_s[:]
+            )
             r = stats.tile([P, 1], F32, name="r")
-            nc.vector.reciprocal(r[:], rms[:])
+            nc.scalar.activation(r[:], mean_s[:], ACT.Abs_reciprocal_sqrt, bias=mean_v_eps[:])
             result = work.tile([P, PICKED], F32, name="result")
-            nc.vector.tensor_scalar_mul(result[:], picked[:], r[:])
+            nc.scalar.activation(result[:], picked[:], ACT.Copy, scale=r[:])
             nc.sync.dma_start(out[b * P : (b + 1) * P, :], result[:])

@@ -35,6 +35,12 @@ def tile_qllamadecoderlayer_kernel(tc, x, lnw, offs, out):
             nc.sync.dma_start(block[:], x[b * P : (b + 1) * P, :])
             blocks.append(block)
 
+        def scale_and_store(b, picked, r):
+            result = work.tile([P, PICKED], F32, name="result")
+            nc.scalar.activation(result[:], picked[:], ACT.Copy, scale=r[:])
+            nc.sync.dma_start(out[b * P : (b + 1) * P, :], result[:])
+
+        waiting = None
         for b in range(BLOCKS):
             block = blocks[b]
             squares_v = scratch.tile([P, VECTOR_SHARE], F32, name="squares_v")
@@ -53,8 +59,9 @@ def tile_qllamadecoderlayer_kernel(tc, x, lnw, offs, out):
             nc.scalar.activation(
                 squares_s[:], block[:, :SCALAR_SHARE], ACT.Square, scale=1.0 / 32.0, accum_out=mean_s[:]
             )
+            if waiting is not None:
+                scale_and_store(b - 1, *waiting)
             r = stats.tile([P, 1], F32, name="r")
             nc.scalar.activation(r[:], mean_s[:], ACT.Abs_reciprocal_sqrt, bias=mean_v_eps[:])
-            result = work.tile([P, PICKED], F32, name="result")
-            nc.scalar.activation(result[:], picked[:], ACT.Copy, scale=r[:])
-            nc.sync.dma_start(out[b * P : (b + 1) * P, :], result[:])
+            waiting = (picked, r)
+        scale_and_store(BLOCKS - 1, *waiting)

@@ -11,7 +11,7 @@ CHANNELS = 1024
 PICKED = 128
 BLOCKS = TOKENS // P
 EPS = 1e-5
-SCALAR_SHARE = 5 * CHANNELS // 8
+SCALAR_SHARE = 1 * CHANNELS // 2
 VECTOR_SHARE = CHANNELS - SCALAR_SHARE
 
 
@@ -35,12 +35,6 @@ def tile_qllamadecoderlayer_kernel(tc, x, lnw, offs, out):
             nc.sync.dma_start(block[:], x[b * P : (b + 1) * P, :])
             blocks.append(block)
 
-        def scale_and_store(b, picked, r):
-            result = work.tile([P, PICKED], F32, name="result")
-            nc.scalar.activation(result[:], picked[:], ACT.Copy, scale=r[:])
-            nc.sync.dma_start(out[b * P : (b + 1) * P, :], result[:])
-
-        waiting = None
         for b in range(BLOCKS):
             block = blocks[b]
             squares_v = scratch.tile([P, VECTOR_SHARE], F32, name="squares_v")
@@ -59,9 +53,8 @@ def tile_qllamadecoderlayer_kernel(tc, x, lnw, offs, out):
             nc.scalar.activation(
                 squares_s[:], block[:, :SCALAR_SHARE], ACT.Square, scale=1.0 / 32.0, accum_out=mean_s[:]
             )
-            if waiting is not None:
-                scale_and_store(b - 1, *waiting)
             r = stats.tile([P, 1], F32, name="r")
             nc.scalar.activation(r[:], mean_s[:], ACT.Abs_reciprocal_sqrt, bias=mean_v_eps[:])
-            waiting = (picked, r)
-        scale_and_store(BLOCKS - 1, *waiting)
+            result = work.tile([P, PICKED], F32, name="result")
+            nc.scalar.activation(result[:], picked[:], ACT.Copy, scale=r[:])
+            nc.sync.dma_start(out[b * P : (b + 1) * P, :], result[:])

@@ -11,8 +11,8 @@ CHANNELS = 1024
 PICKED = 128
 BLOCKS = TOKENS // P
 EPS = 1e-5
-SCALAR_SHARE = 1 * CHANNELS // 2
-VECTOR_SHARE = CHANNELS - SCALAR_SHARE
+HALF = CHANNELS // 2
+LAST = BLOCKS - 1
 
 
 def tile_qllamadecoderlayer_kernel(tc, x, lnw, offs, out):
@@ -32,27 +32,29 @@ def tile_qllamadecoderlayer_kernel(tc, x, lnw, offs, out):
         blocks = []
         for b in range(BLOCKS):
             block = tokens.tile([P, CHANNELS], F32, name="block")
-            nc.sync.dma_start(block[:], x[b * P : (b + 1) * P, :])
+            rows = x[b * P : (b + 1) * P, :]
+            if b < LAST:
+                nc.sync.dma_start(block[:], rows)
+            else:
+                nc.sync.dma_start(block[:, :HALF], rows[:, :HALF])
+                nc.sync.dma_start(block[:, HALF:], rows[:, HALF:])
             blocks.append(block)
 
         for b in range(BLOCKS):
             block = blocks[b]
-            squares_v = scratch.tile([P, VECTOR_SHARE], F32, name="squares_v")
+            squares_v = scratch.tile([P, HALF], F32, name="squares_v")
             mean_v = stats.tile([P, 1], F32, name="mean_v")
             nc.vector.scalar_tensor_tensor(
-                squares_v[:], block[:, SCALAR_SHARE:], 1.0 / CHANNELS, block[:, SCALAR_SHARE:], MULT, MULT,
-                accum_out=mean_v[:],
+                squares_v[:], block[:, :HALF], 1.0 / CHANNELS, block[:, :HALF], MULT, MULT, accum_out=mean_v[:]
             )
             mean_v_eps = stats.tile([P, 1], F32, name="mean_v_eps")
             nc.vector.tensor_scalar_add(mean_v_eps[:], mean_v[:], EPS)
             picked = work.tile([P, PICKED], F32, name="picked")
             nc.vector.tensor_tensor(picked[:], block[:].indirect(offsets[:]), gain[:], MULT)
 
-            squares_s = scratch.tile([P, SCALAR_SHARE], F32, name="squares_s")
+            squares_s = scratch.tile([P, HALF], F32, name="squares_s")
             mean_s = stats.tile([P, 1], F32, name="mean_s")
-            nc.scalar.activation(
-                squares_s[:], block[:, :SCALAR_SHARE], ACT.Square, scale=1.0 / 32.0, accum_out=mean_s[:]
-            )
+            nc.scalar.activation(squares_s[:], block[:, HALF:], ACT.Square, scale=1.0 / 32.0, accum_out=mean_s[:])
             r = stats.tile([P, 1], F32, name="r")
             nc.scalar.activation(r[:], mean_s[:], ACT.Abs_reciprocal_sqrt, bias=mean_v_eps[:])
             result = work.tile([P, PICKED], F32, name="result")

@@ -13,6 +13,7 @@ BLOCKS = TOKENS // P
 EPS = 1e-5
 HALF = CHANNELS // 2
 LAST = BLOCKS - 1
+STORE_AFTER = {3: 4, 5: 2, 6: 1, 7: 1}
 
 
 def tile_qllamadecoderlayer_kernel(tc, x, lnw, offs, out):
@@ -29,10 +30,14 @@ def tile_qllamadecoderlayer_kernel(tc, x, lnw, offs, out):
         gain = held.tile([P, PICKED], F32, name="gain")
         nc.scalar.dma_start(gain[:], lnw.broadcast_to([P, PICKED]))
 
+        x_by_block = x.rearrange("(p b) c -> p b c", b=BLOCKS)
+        out_by_partition = out.rearrange("(p b) j -> p (b j)", b=BLOCKS)
+        results = held.tile([P, BLOCKS * PICKED], F32, name="results")
+
         blocks = []
         for b in range(BLOCKS):
             block = tokens.tile([P, CHANNELS], F32, name="block")
-            rows = x[b * P : (b + 1) * P, :]
+            rows = x_by_block[:, b, :]
             if b < LAST:
                 nc.sync.dma_start(block[:], rows)
             else:
@@ -57,6 +62,7 @@ def tile_qllamadecoderlayer_kernel(tc, x, lnw, offs, out):
             nc.scalar.activation(squares_s[:], block[:, HALF:], ACT.Square, scale=1.0 / 32.0, accum_out=mean_s[:])
             r = stats.tile([P, 1], F32, name="r")
             nc.scalar.activation(r[:], mean_s[:], ACT.Abs_reciprocal_sqrt, bias=mean_v_eps[:])
-            result = work.tile([P, PICKED], F32, name="result")
-            nc.scalar.activation(result[:], picked[:], ACT.Copy, scale=r[:])
-            nc.sync.dma_start(out[b * P : (b + 1) * P, :], result[:])
+            nc.scalar.activation(results[:, b * PICKED : (b + 1) * PICKED], picked[:], ACT.Copy, scale=r[:])
+            if b in STORE_AFTER:
+                columns = slice((b + 1 - STORE_AFTER[b]) * PICKED, (b + 1) * PICKED)
+                nc.sync.dma_start(out_by_partition[:, columns], results[:, columns])

@@ -13,6 +13,7 @@ BLOCKS = TOKENS // P
 EPS = 1e-5
 HALF = CHANNELS // 2
 LAST = BLOCKS - 1
+ROWS = 32
 STORE_AFTER = {3: 4, 5: 2, 6: 1, 7: 1}
 
 
@@ -24,11 +25,19 @@ def tile_qllamadecoderlayer_kernel(tc, x, lnw, offs, out):
         tc.tile_pool(name="scratch", bufs=2) as scratch,
         tc.tile_pool(name="work", bufs=BLOCKS) as work,
         tc.tile_pool(name="stats", bufs=BLOCKS) as stats,
+        tc.psum_pool(name="psum", bufs=1) as psum,
     ):
         offsets = held.tile([P, PICKED // 16], U16, name="offsets")
         nc.sync.dma_start(offsets[:], offs)
+        lnw_rows = held.tile([ROWS, PICKED], F32, name="lnw_rows")
+        nc.scalar.dma_start(lnw_rows[:], lnw.broadcast_to([ROWS, PICKED]))
+        first_row = held.tile([ROWS, P], F32, name="first_row")
+        nc.gpsimd.memset(first_row[:], 0.0)
+        nc.gpsimd.memset(first_row[0:1, :], 1.0)
+        gain_psum = psum.tile([P, PICKED], F32, name="gain_psum")
+        nc.tensor.matmul(gain_psum[:], first_row[:], lnw_rows[:], start=True, stop=True)
         gain = held.tile([P, PICKED], F32, name="gain")
-        nc.scalar.dma_start(gain[:], lnw.broadcast_to([P, PICKED]))
+        nc.scalar.copy(gain[:], gain_psum[:])
 
         x_by_block = x.rearrange("(p b) c -> p b c", b=BLOCKS)
         out_by_partition = out.rearrange("(p b) j -> p (b j)", b=BLOCKS)

@@ -27,17 +27,17 @@ def tile_qllamadecoderlayer_kernel(tc, x, lnw, offs, out):
         tc.tile_pool(name="stats", bufs=BLOCKS) as stats,
         tc.psum_pool(name="psum", bufs=1) as psum,
     ):
+        lnw_rows = held.tile([ROWS, PICKED], F32, name="lnw_rows")
+        nc.sync.dma_start(lnw_rows[:], lnw.broadcast_to([ROWS, PICKED]))
         offsets = held.tile([P, PICKED // 16], U16, name="offsets")
         nc.sync.dma_start(offsets[:], offs)
-        lnw_rows = held.tile([ROWS, PICKED], F32, name="lnw_rows")
-        nc.scalar.dma_start(lnw_rows[:], lnw.broadcast_to([ROWS, PICKED]))
         first_row = held.tile([ROWS, P], F32, name="first_row")
         nc.gpsimd.memset(first_row[:], 0.0)
         nc.gpsimd.memset(first_row[0:1, :], 1.0)
         gain_psum = psum.tile([P, PICKED], F32, name="gain_psum")
         nc.tensor.matmul(gain_psum[:], first_row[:], lnw_rows[:], start=True, stop=True)
         gain = held.tile([P, PICKED], F32, name="gain")
-        nc.scalar.copy(gain[:], gain_psum[:])
+        nc.vector.tensor_copy(gain[:], gain_psum[:])
 
         x_by_block = x.rearrange("(p b) c -> p b c", b=BLOCKS)
         out_by_partition = out.rearrange("(p b) j -> p (b j)", b=BLOCKS)

@@ -47,7 +47,7 @@ def tile_qllamadecoderlayer_kernel(tc, x, lnw, offs, out):
         for b in range(BLOCKS):
             block = tokens.tile([P, CHANNELS], F32, name="block")
             rows = x_by_block[:, b, :]
-            if b < LAST:
+            if 0 < b < LAST:
                 nc.sync.dma_start(block[:], rows)
             else:
                 nc.sync.dma_start(block[:, :HALF], rows[:, :HALF])

@@ -27,6 +27,13 @@ def tile_qllamadecoderlayer_kernel(tc, x, lnw, offs, out):
         tc.tile_pool(name="stats", bufs=BLOCKS) as stats,
         tc.psum_pool(name="psum", bufs=1) as psum,
     ):
+        x_by_block = x.rearrange("(p b) c -> p b c", b=BLOCKS)
+        out_by_partition = out.rearrange("(p b) j -> p (b j)", b=BLOCKS)
+        results = held.tile([P, BLOCKS * PICKED], F32, name="results")
+
+        first_block = tokens.tile([P, CHANNELS], F32, name="block")
+        nc.sync.dma_start(first_block[:, :HALF], x_by_block[:, 0, :HALF])
+
         lnw_rows = held.tile([ROWS, PICKED], F32, name="lnw_rows")
         nc.sync.dma_start(lnw_rows[:], lnw.broadcast_to([ROWS, PICKED]))
         offsets = held.tile([P, PICKED // 16], U16, name="offsets")
@@ -39,15 +46,12 @@ def tile_qllamadecoderlayer_kernel(tc, x, lnw, offs, out):
         gain = held.tile([P, PICKED], F32, name="gain")
         nc.vector.tensor_copy(gain[:], gain_psum[:])
 
-        x_by_block = x.rearrange("(p b) c -> p b c", b=BLOCKS)
-        out_by_partition = out.rearrange("(p b) j -> p (b j)", b=BLOCKS)
-        results = held.tile([P, BLOCKS * PICKED], F32, name="results")
-
-        blocks = []
-        for b in range(BLOCKS):
+        nc.sync.dma_start(first_block[:, HALF:], x_by_block[:, 0, HALF:])
+        blocks = [first_block]
+        for b in range(1, BLOCKS):
             block = tokens.tile([P, CHANNELS], F32, name="block")
             rows = x_by_block[:, b, :]
-            if 0 < b < LAST:
+            if b < LAST:
                 nc.sync.dma_start(block[:], rows)
             else:
                 nc.sync.dma_start(block[:, :HALF], rows[:, :HALF])
@@ -71,7 +75,11 @@ def tile_qllamadecoderlayer_kernel(tc, x, lnw, offs, out):
             nc.scalar.activation(squares_s[:], block[:, HALF:], ACT.Square, scale=1.0 / 32.0, accum_out=mean_s[:])
             r = stats.tile([P, 1], F32, name="r")
             nc.scalar.activation(r[:], mean_s[:], ACT.Abs_reciprocal_sqrt, bias=mean_v_eps[:])
-            nc.scalar.activation(results[:, b * PICKED : (b + 1) * PICKED], picked[:], ACT.Copy, scale=r[:])
+            result = results[:, b * PICKED : (b + 1) * PICKED]
+            if b < LAST:
+                nc.scalar.activation(result, picked[:], ACT.Copy, scale=r[:])
+            else:
+                nc.vector.tensor_scalar_mul(result, picked[:], r[:])
             if b in STORE_AFTER:
                 columns = slice((b + 1 - STORE_AFTER[b]) * PICKED, (b + 1) * PICKED)
                 nc.sync.dma_start(out_by_partition[:, columns], results[:, columns])

@@ -27,9 +27,9 @@ def tile_qllamadecoderlayer_kernel(tc, x, lnw, offs, out):
         tc.tile_pool(name="stats", bufs=BLOCKS) as stats,
         tc.psum_pool(name="psum", bufs=1) as psum,
     ):
-        x_by_block = x.rearrange("(p b) c -> p b c", b=BLOCKS)
-        out_by_partition = out.rearrange("(p b) j -> p (b j)", b=BLOCKS)
-        results = held.tile([P, BLOCKS * PICKED], F32, name="results")
+        x_by_block = x.rearrange("(b p) c -> p b c", b=BLOCKS)
+        out_by_block = out.rearrange("(b p) j -> p b j", b=BLOCKS)
+        results = held.tile([P, BLOCKS, PICKED], F32, name="results")
 
         first_block = tokens.tile([P, CHANNELS], F32, name="block")
         nc.sync.dma_start(first_block[:, :HALF], x_by_block[:, 0, :HALF])
@@ -75,11 +75,11 @@ def tile_qllamadecoderlayer_kernel(tc, x, lnw, offs, out):
             nc.scalar.activation(squares_s[:], block[:, HALF:], ACT.Square, scale=1.0 / 32.0, accum_out=mean_s[:])
             r = stats.tile([P, 1], F32, name="r")
             nc.scalar.activation(r[:], mean_s[:], ACT.Abs_reciprocal_sqrt, bias=mean_v_eps[:])
-            result = results[:, b * PICKED : (b + 1) * PICKED]
-            if b < LAST:
+            result = results[:, b, :]
+            if b < LAST - 1:
                 nc.scalar.activation(result, picked[:], ACT.Copy, scale=r[:])
             else:
                 nc.vector.tensor_scalar_mul(result, picked[:], r[:])
             if b in STORE_AFTER:
-                columns = slice((b + 1 - STORE_AFTER[b]) * PICKED, (b + 1) * PICKED)
-                nc.sync.dma_start(out_by_partition[:, columns], results[:, columns])
+                stored = slice(b + 1 - STORE_AFTER[b], b + 1)
+                nc.sync.dma_start(out_by_block[:, stored, :], results[:, stored, :])

@@ -4,6 +4,7 @@ F32 = mybir.dt.float32
 U16 = mybir.dt.uint16
 ACT = mybir.ActivationFunctionType
 MULT = mybir.AluOpType.mult
+ADD = mybir.AluOpType.add
 
 P = 128
 TOKENS = 1024
@@ -12,6 +13,7 @@ PICKED = 128
 BLOCKS = TOKENS // P
 EPS = 1e-5
 HALF = CHANNELS // 2
+LAST_SHARE = HALF * 3 // 4
 LAST = BLOCKS - 1
 ROWS = 32
 STORE_AFTER = {3: 4, 5: 2, 6: 1, 7: 1}
@@ -60,13 +62,22 @@ def tile_qllamadecoderlayer_kernel(tc, x, lnw, offs, out):
 
         for b in range(BLOCKS):
             block = blocks[b]
-            squares_v = scratch.tile([P, HALF], F32, name="squares_v")
+            vector_share = HALF if b < LAST else LAST_SHARE
+            squares_v = scratch.tile([P, vector_share], F32, name="squares_v")
             mean_v = stats.tile([P, 1], F32, name="mean_v")
             nc.vector.scalar_tensor_tensor(
-                squares_v[:], block[:, :HALF], 1.0 / CHANNELS, block[:, :HALF], MULT, MULT, accum_out=mean_v[:]
+                squares_v[:], block[:, :vector_share], 1.0 / CHANNELS, block[:, :vector_share], MULT, MULT, accum_out=mean_v[:]
             )
             mean_v_eps = stats.tile([P, 1], F32, name="mean_v_eps")
-            nc.vector.tensor_scalar_add(mean_v_eps[:], mean_v[:], EPS)
+            if b < LAST:
+                nc.vector.tensor_scalar_add(mean_v_eps[:], mean_v[:], EPS)
+            else:
+                squares_early = scratch.tile([P, HALF - LAST_SHARE], F32, name="squares_early")
+                mean_early = stats.tile([P, 1], F32, name="mean_early")
+                nc.scalar.activation(
+                    squares_early[:], block[:, LAST_SHARE:HALF], ACT.Square, scale=1.0 / 32.0, accum_out=mean_early[:]
+                )
+                nc.vector.scalar_tensor_tensor(mean_v_eps[:], mean_v[:], EPS, mean_early[:], ADD, ADD)
             picked = work.tile([P, PICKED], F32, name="picked")
             nc.vector.tensor_tensor(picked[:], block[:].indirect(offsets[:]), gain[:], MULT)
 

@@ -40,6 +40,10 @@ def tile_qllamadecoderlayer_kernel(tc, x, lnw, offs, out):
         nc.sync.dma_start(lnw_rows[:], lnw.broadcast_to([ROWS, PICKED]))
         offsets = held.tile([P, PICKED // 16], U16, name="offsets")
         nc.sync.dma_start(offsets[:], offs)
+        ones = held.tile([P, 1], F32, name="ones")
+        nc.vector.memset(ones[:], 1.0)
+        unread_root = held.tile([P, 1], F32, name="unread_root")
+        nc.scalar.activation(unread_root[:], ones[:], ACT.Abs_reciprocal_sqrt)
         first_row = held.tile([ROWS, P], F32, name="first_row")
         nc.gpsimd.memset(first_row[:], 0.0)
         nc.gpsimd.memset(first_row[0:1, :], 1.0)

import concourse.mybir as mybir

F32 = mybir.dt.float32
U16 = mybir.dt.uint16
ACT = mybir.ActivationFunctionType
MULT = mybir.AluOpType.mult
ADD = mybir.AluOpType.add

P = 128
TOKENS = 1024
CHANNELS = 1024
PICKED = 128
BLOCKS = TOKENS // P
EPS = 1e-5
HALF = CHANNELS // 2
LAST_SHARE = HALF * 3 // 4
LAST = BLOCKS - 1
ROWS = 32
STORE_AFTER = {3: 4, 5: 2, 6: 1, 7: 1}


def tile_qllamadecoderlayer_kernel(tc, x, lnw, offs, out):
    nc = tc.nc
    with (
        tc.tile_pool(name="held", bufs=1) as held,
        tc.tile_pool(name="tokens", bufs=BLOCKS) as tokens,
        tc.tile_pool(name="scratch", bufs=2) as scratch,
        tc.tile_pool(name="work", bufs=BLOCKS) as work,
        tc.tile_pool(name="stats", bufs=BLOCKS) as stats,
        tc.psum_pool(name="psum", bufs=1) as psum,
    ):
        x_by_block = x.rearrange("(b p) c -> p b c", b=BLOCKS)
        out_by_block = out.rearrange("(b p) j -> p b j", b=BLOCKS)
        results = held.tile([P, BLOCKS, PICKED], F32, name="results")

        first_block = tokens.tile([P, CHANNELS], F32, name="block")
        nc.sync.dma_start(first_block[:, :HALF], x_by_block[:, 0, :HALF])

        lnw_rows = held.tile([ROWS, PICKED], F32, name="lnw_rows")
        nc.sync.dma_start(lnw_rows[:], lnw.broadcast_to([ROWS, PICKED]))
        offsets = held.tile([P, PICKED // 16], U16, name="offsets")
        nc.sync.dma_start(offsets[:], offs)
        ones = held.tile([P, 1], F32, name="ones")
        nc.vector.memset(ones[:], 1.0)
        unread_root = held.tile([P, 1], F32, name="unread_root")
        nc.scalar.activation(unread_root[:], ones[:], ACT.Abs_reciprocal_sqrt)
        first_row = held.tile([ROWS, P], F32, name="first_row")
        nc.gpsimd.memset(first_row[:], 0.0)
        nc.gpsimd.memset(first_row[0:1, :], 1.0)
        gain_psum = psum.tile([P, PICKED], F32, name="gain_psum")
        nc.tensor.matmul(gain_psum[:], first_row[:], lnw_rows[:], start=True, stop=True)
        gain = held.tile([P, PICKED], F32, name="gain")
        nc.vector.tensor_copy(gain[:], gain_psum[:])

        nc.sync.dma_start(first_block[:, HALF:], x_by_block[:, 0, HALF:])
        blocks = [first_block]
        for b in range(1, BLOCKS):
            block = tokens.tile([P, CHANNELS], F32, name="block")
            rows = x_by_block[:, b, :]
            if b < LAST:
                nc.sync.dma_start(block[:], rows)
            else:
                nc.sync.dma_start(block[:, :HALF], rows[:, :HALF])
                nc.sync.dma_start(block[:, HALF:], rows[:, HALF:])
            blocks.append(block)

        for b in range(BLOCKS):
            block = blocks[b]
            vector_share = HALF if b < LAST else LAST_SHARE
            squares_v = scratch.tile([P, vector_share], F32, name="squares_v")
            mean_v = stats.tile([P, 1], F32, name="mean_v")
            nc.vector.scalar_tensor_tensor(
                squares_v[:], block[:, :vector_share], 1.0 / CHANNELS, block[:, :vector_share], MULT, MULT, accum_out=mean_v[:]
            )
            mean_v_eps = stats.tile([P, 1], F32, name="mean_v_eps")
            if b < LAST:
                nc.vector.tensor_scalar_add(mean_v_eps[:], mean_v[:], EPS)
            else:
                squares_early = scratch.tile([P, HALF - LAST_SHARE], F32, name="squares_early")
                mean_early = stats.tile([P, 1], F32, name="mean_early")
                nc.scalar.activation(
                    squares_early[:], block[:, LAST_SHARE:HALF], ACT.Square, scale=1.0 / 32.0, accum_out=mean_early[:]
                )
                nc.vector.scalar_tensor_tensor(mean_v_eps[:], mean_v[:], EPS, mean_early[:], ADD, ADD)
            picked = work.tile([P, PICKED], F32, name="picked")
            nc.vector.tensor_tensor(picked[:], block[:].indirect(offsets[:]), gain[:], MULT)

            squares_s = scratch.tile([P, HALF], F32, name="squares_s")
            mean_s = stats.tile([P, 1], F32, name="mean_s")
            nc.scalar.activation(squares_s[:], block[:, HALF:], ACT.Square, scale=1.0 / 32.0, accum_out=mean_s[:])
            r = stats.tile([P, 1], F32, name="r")
            nc.scalar.activation(r[:], mean_s[:], ACT.Abs_reciprocal_sqrt, bias=mean_v_eps[:])
            result = results[:, b, :]
            if b < LAST - 1:
                nc.scalar.activation(result, picked[:], ACT.Copy, scale=r[:])
            else:
                nc.vector.tensor_scalar_mul(result, picked[:], r[:])
            if b in STORE_AFTER:
                stored = slice(b + 1 - STORE_AFTER[b], b + 1)
                nc.sync.dma_start(out_by_block[:, stored, :], results[:, stored, :])
